import numpy as np
import ml_dtypes


def mxq(x, axis, fmt="e4m3"):
    dtype, down = {"e4m3": (ml_dtypes.float8_e4m3fn, 7), "e5m2": (ml_dtypes.float8_e5m2, 14)}[fmt]
    v = np.moveaxis(np.asarray(x, np.float32).astype(ml_dtypes.bfloat16).astype(np.float64), axis, -1)
    blocks = v.reshape(v.shape[:-1] + (-1, 32))
    amax = np.abs(blocks).max(-1, keepdims=True)
    byte = np.maximum(np.where(amax > 0, np.frexp(amax)[1] - 1 + 127, 0) - down, 1)
    scale = np.exp2(byte - 127.0)
    codes = (blocks / scale).astype(np.float32).astype(dtype).astype(np.float64)
    return np.moveaxis((codes * scale).reshape(v.shape), -1, axis)


WIDE = False


def mx_kscale(k):
    if not WIDE:
        return np.ones(k)
    levels = np.array([10, -10, 5, -5, 0])
    a = np.random.permutation(np.resize(levels, k // 512 * 4)).reshape(k // 512, 4)
    idx = np.arange(k)
    return np.exp2(a[idx // 512, idx % 128 // 32])


BF16 = ml_dtypes.bfloat16


def bf(x):
    return np.asarray(x, np.float32).astype(BF16)


def f64(x):
    return np.asarray(x).astype(np.float64)


E2M1 = np.array([0.0, 0.5, 1.0, 1.5, 2.0, 3.0, 4.0, 6.0, -0.0, -0.5, -1.0, -1.5, -2.0, -3.0, -4.0, -6.0])


def pack_weight(w, fmt):
    k, n = w.shape
    w = f64(bf(w)).reshape(k // 32, 32, n)
    amax = np.abs(w).max(1)
    if fmt == "e4m3":
        byte = np.frexp(amax)[1] - 1 + 127 - 7
    else:
        mant, ex = np.frexp(amax / 6.0)
        byte = np.where(mant > 0.5, ex, ex - 1) + 127
    byte = np.clip(np.where(amax > 0, byte, 1), 1, 254)
    scaled = (w * np.exp2(127.0 - byte)[:, None, :]).reshape(k, n).astype(np.float32)
    by_word = np.ascontiguousarray(scaled.reshape(k // 512, 128, 4, n).transpose(0, 1, 3, 2))
    if fmt == "e4m3":
        words = by_word.astype(ml_dtypes.float8_e4m3fn).view(np.uint8)
    else:
        c = by_word.astype(ml_dtypes.float4_e2m1fn).view(np.uint8) & 0xF
        words = c[..., 0::2] | (c[..., 1::2] << 4)
    return np.ascontiguousarray(words), np.ascontiguousarray(byte.astype(np.uint8).reshape(k // 512, 16, n))


def unpack_weight(words, scales, fmt):
    g, p, n, _ = words.shape
    if fmt == "e4m3":
        vals = np.ascontiguousarray(words).view(ml_dtypes.float8_e4m3fn).astype(np.float64)
    else:
        nib = np.empty((g, p, n, 4), np.uint8)
        nib[..., 0::2] = words & 0xF
        nib[..., 1::2] = words >> 4
        vals = E2M1[nib]
    vals = vals * np.repeat(np.exp2(scales.astype(np.float64) - 127.0), 8, axis=1)[..., None]
    return vals.transpose(0, 1, 3, 2).reshape(g * 512, n)

def pack4(w):
    words, scales = pack_weight(w, "e2m1")
    return words.reshape(words.shape[0], 128, -1), scales


def unpack4(words, scales):
    return unpack_weight(words.reshape(words.shape[0], 128, -1, 2), scales, "e2m1")


B, S, D, H, HKV, HD, WINDOW, KB = 1, 4096, 1024, 8, 1, 128, 256, 512
EPS = 1e-6
THETA = 10000.0


def rope_tables():
    inv_freq = 1.0 / THETA ** (np.arange(0, HD, 2) / HD)
    ang = np.arange(S)[:, None] * inv_freq[None, :]
    emb = np.concatenate([ang, ang], axis=-1)
    return np.broadcast_to(np.cos(emb)[None], (B, S, HD)), np.broadcast_to(np.sin(emb)[None], (B, S, HD))


def rms_norm(x, gain):
    var = np.mean(x * x, axis=-1, keepdims=True)
    return x * (1.0 / np.sqrt(var + EPS)) * gain


def rotate_half(x):
    return np.concatenate([-x[..., HD // 2:], x[..., :HD // 2]], axis=-1)


def apply_rope(x, cos, sin):
    return x * cos[:, :, None, :] + rotate_half(x) * sin[:, :, None, :]


def setup_inputs():
    s = mx_kscale(D)
    cos, sin = rope_tables()
    hidden_states = bf(np.random.standard_normal((B, S, D)) * s)
    Wq_words, Wq_scales = pack4(np.random.standard_normal((D, H * HD)) / np.sqrt(D) / s[:, None])
    Wk_words, Wk_scales = pack4(np.random.standard_normal((D, HKV * HD)) / np.sqrt(D) / s[:, None])
    Wv_words, Wv_scales = pack4(np.random.standard_normal((D, HKV * HD)) * 2.0 / np.sqrt(D) / s[:, None])
    q_scale = bf(np.random.uniform(0.5, 1.5, HD))
    k_scale = bf(np.random.uniform(0.5, 1.5, HD))
    return {
        "hidden_states": hidden_states,
        "cos": bf(cos),
        "sin": bf(sin),
        "Wq_words": Wq_words,
        "Wq_scales": Wq_scales,
        "Wk_words": Wk_words,
        "Wk_scales": Wk_scales,
        "Wv_words": Wv_words,
        "Wv_scales": Wv_scales,
        "q_scale": q_scale,
        "k_scale": k_scale,
    }


def reference(hidden_states, cos, sin, Wq_words, Wq_scales, Wk_words, Wk_scales, Wv_words, Wv_scales, q_scale, k_scale):
    xq = mxq(f64(hidden_states), 2, "e4m3")
    q = (xq @ unpack4(Wq_words, Wq_scales)).reshape(B, S, H, HD)
    k = (xq @ unpack4(Wk_words, Wk_scales)).reshape(B, S, HKV, HD)
    v = (xq @ unpack4(Wv_words, Wv_scales)).reshape(B, S, HKV, HD)
    q = rms_norm(q, f64(q_scale))
    k = rms_norm(k, f64(k_scale))
    q = apply_rope(q, f64(cos), f64(sin))
    k = apply_rope(k, f64(cos), f64(sin))
    return q, k, v

@@ -1,0 +1,241 @@
+from contextlib import ExitStack
+
+import concourse.mybir as mybir
+from concourse.masks import make_identity
+
+F32 = mybir.dt.float32
+BF16 = mybir.dt.bfloat16
+I32 = mybir.dt.int32
+U32 = mybir.dt.uint32
+U8 = mybir.dt.uint8
+FP8X4 = mybir.dt.float8_e4m3fn_x4
+FP4X4 = mybir.dt.float4_e2m1fn_x4
+ALU = mybir.AluOpType
+ACT = mybir.ActivationFunctionType
+
+P = 128
+S = 4096
+D = 1024
+HD = 128
+HALF = HD // 2
+Q_HEADS = 8
+ROPE_HEADS = Q_HEADS + 1
+OUT_HEADS = ROPE_HEADS + 1
+N_ALL = OUT_HEADS * HD
+K_PASS = 512
+PASSES = D // K_PASS
+TILES = S // P
+CHUNK = 4
+PAIR = 2
+EPS = 1e-6
+
+FLOPS = 2 * S * D * N_ALL
+
+
+def tile_multiheadattention_pa_t_kernel(
+    tc,
+    hidden_states,
+    cos,
+    sin,
+    Wq_words,
+    Wq_scales,
+    Wk_words,
+    Wk_scales,
+    Wv_words,
+    Wv_scales,
+    q_scale,
+    k_scale,
+    out_0,
+    out_1,
+    out_2,
+):
+    nc = tc.nc
+
+    x_dram = hidden_states.rearrange("b (p t) k -> (b p) t k", t=TILES)
+    cos_dram = cos.rearrange("b (p t) d -> (b p) t d", t=TILES)
+    sin_dram = sin.rearrange("b (p t) d -> (b p) t d", t=TILES)
+    q_dram = out_0.rearrange("b (p t) h d -> (b p) t (h d)", t=TILES)
+    k_dram = out_1.rearrange("b (p t) h d -> (b p) t (h d)", t=TILES)
+    v_dram = out_2.rearrange("b (p t) h d -> (b p) t (h d)", t=TILES)
+
+    with ExitStack() as ctx:
+        keep = ctx.enter_context(tc.tile_pool(name="keep", bufs=1))
+        tables = ctx.enter_context(tc.tile_pool(name="tables", bufs=2))
+        quant = ctx.enter_context(tc.tile_pool(name="quant", bufs=3))
+        stats = ctx.enter_context(tc.tile_pool(name="stats", bufs=3))
+        work = ctx.enter_context(tc.tile_pool(name="work", bufs=3))
+        psum = ctx.enter_context(tc.psum_pool(name="psum", bufs=2))
+        ctx.enter_context(tc.manual_schedule())
+
+        w_scales = keep.tile([P, PASSES, N_ALL], U8, align_bytes=64)
+        nc.vector.memset(w_scales[:].rearrange("p g n -> p (g n)").bitcast(I32), 0)
+        eps = keep.tile([P, 1], F32)
+        nc.vector.memset(eps[:], EPS)
+        ident = keep.tile([P, P], F32)
+        make_identity(nc, ident[:])
+
+        x_chunks = []
+        cos_chunks = []
+        sin_chunks = []
+        for c in range(TILES // CHUNK):
+            x_chunks.append(keep.tile([P, CHUNK, D], BF16, name="x%d" % c))
+            cos_chunks.append(keep.tile([P, CHUNK, HD], BF16, name="cos%d" % c))
+            sin_chunks.append(keep.tile([P, CHUNK, HD], BF16, name="sin%d" % c))
+
+        def load_chunk(c):
+            rows = slice(c * CHUNK, (c + 1) * CHUNK)
+            nc.sync.dma_start(out=x_chunks[c][:], in_=x_dram[:, rows, :])
+            nc.sync.dma_start(out=cos_chunks[c][:], in_=cos_dram[:, rows, :])
+            nc.sync.dma_start(out=sin_chunks[c][:], in_=sin_dram[:, rows, :])
+
+        load_chunk(0)
+
+        w_words = keep.tile([P, PASSES, 2 * N_ALL], U8, align_bytes=64)
+        col = 0
+        for words, scales in ((Wq_words, Wq_scales), (Wk_words, Wk_scales), (Wv_words, Wv_scales)):
+            width = scales.shape[2]
+            nc.sync.dma_start(
+                out=w_words[:, :, 2 * col : 2 * (col + width)].bitcast(I32),
+                in_=words.rearrange("g p b -> p g b").bitcast(I32),
+            )
+            for quad in range(4):
+                nc.sync.dma_start(
+                    out=w_scales[32 * quad : 32 * quad + 4, :, col : col + width].bitcast(I32),
+                    in_=scales[:, 4 * quad : 4 * quad + 4, :].rearrange("g r n -> r g n").bitcast(I32),
+                )
+            col += width
+
+        gains = keep.tile([P, 2, HD], BF16)
+        nc.scalar.dma_start(out=gains[:, 0, :], in_=q_scale.partition_broadcast(P))
+        nc.scalar.dma_start(out=gains[:, 1, :], in_=k_scale.partition_broadcast(P))
+
+        for c in range(1, TILES // CHUNK):
+            load_chunk(c)
+
+        x_codes = {}
+        x_scales = {}
+        banks = {}
+        rstds = {}
+        rope_tables = {}
+        results = {}
+
+        def quantise(t):
+            x_words = x_chunks[t // CHUNK][:, t % CHUNK, :].bitcast(F32)
+            xt = psum.tile([P, PASSES * 2, P], F32, tag="xt")
+            for g in range(PASSES):
+                for u in range(2):
+                    nc.tensor.transpose(
+                        xt[:, 2 * g + u, :], x_words[:, 256 * g + u : 256 * (g + 1) : 2], ident[:]
+                    )
+            grouped = quant.tile([P, PASSES, P, 2], F32, align_bytes=64)
+            nc.scalar.copy(out=grouped[:], in_=xt[:].rearrange("p (g u) r -> p g r u", u=2))
+            codes = quant.tile([P, PASSES * P], U32, align_bytes=64)
+            scales = quant.tile([P, PASSES * P], U8, align_bytes=64)
+            nc.vector.quantize_mx(
+                out=codes[:].bitcast(FP8X4),
+                scales=scales[:],
+                in_=grouped[:].rearrange("p g r u -> p (g r u)").bitcast(BF16),
+            )
+            x_codes[t] = codes
+            x_scales[t] = scales
+
+        def project(t):
+            qa = psum.tile([P, 4, HD], F32, tag="qa")
+            qb = psum.tile([P, 4, HD], F32, tag="qb")
+            kv = psum.tile([P, 4, HD], F32, tag="kv")
+            groups = (
+                (qa[:].rearrange("p h d -> p (h d)"), 0, 512),
+                (qb[:].rearrange("p h d -> p (h d)"), 512, 512),
+                (kv[:, 0, :], 1024, HD),
+                (kv[:, 1, :], 1152, HD),
+            )
+            for acc, first, width in groups:
+                for g in range(PASSES):
+                    tokens = slice(g * P, (g + 1) * P)
+                    nc.tensor.matmul_mx(
+                        out=acc,
+                        lhsT=x_codes[t][:, tokens].bitcast(FP8X4),
+                        lhsT_scale=x_scales[t][:, tokens],
+                        rhs=w_words[:, g, 2 * first : 2 * (first + width)].bitcast(FP4X4),
+                        rhs_scale=w_scales[:, g, first : first + width],
+                        start=(g == 0),
+                        stop=(g == PASSES - 1),
+                    )
+            banks[t] = [qa[:, h, :] for h in range(4)] + [qb[:, h, :] for h in range(4)] + [kv[:, 0, :], kv[:, 1, :]]
+
+        def norms(t):
+            if t % PAIR == 0:
+                result = work.tile([P, PAIR, OUT_HEADS, HD], F32, tag="result")
+                results[t // PAIR] = result
+            sumsq = stats.tile([P, ROPE_HEADS], F32)
+            for h in range(ROPE_HEADS):
+                squares = stats.tile([P, HD], F32)
+                nc.scalar.activation(out=squares[:], in_=banks[t][h], func=ACT.Square, accum_out=sumsq[:, h : h + 1])
+            nc.scalar.copy(out=results[t // PAIR][:, t % PAIR, ROPE_HEADS, :], in_=banks[t][ROPE_HEADS])
+            rms = stats.tile([P, ROPE_HEADS], F32)
+            nc.scalar.activation(out=rms[:], in_=sumsq[:], func=ACT.Sqrt, scale=1.0 / HD, bias=eps[:, 0:1])
+            rstds[t] = rms
+
+        def build_tables(c):
+            table = tables.tile([P, CHUNK, 2, 2, HD], F32)
+            shape = [P, CHUNK, 2, HD]
+            nc.vector.tensor_tensor(
+                out=table[:, :, :, 0, :],
+                in0=cos_chunks[c][:].unsqueeze(2).to_broadcast(shape),
+                in1=gains[:].unsqueeze(1).to_broadcast(shape),
+                op=ALU.mult,
+            )
+            shape = [P, CHUNK, 2, HALF]
+            for mine, other in ((slice(0, HALF), slice(HALF, HD)), (slice(HALF, HD), slice(0, HALF))):
+                nc.vector.tensor_tensor(
+                    out=table[:, :, :, 1, mine],
+                    in0=sin_chunks[c][:, :, other].unsqueeze(2).to_broadcast(shape),
+                    in1=gains[:, :, mine].unsqueeze(1).to_broadcast(shape),
+                    op=ALU.mult,
+                )
+            rope_tables[c] = table
+
+        def rope(t):
+            if t % CHUNK == 0:
+                build_tables(t // CHUNK)
+            rstd = stats.tile([P, ROPE_HEADS], F32)
+            nc.vector.reciprocal(out=rstd[:], in_=rstds[t][:])
+            products = work.tile([P, ROPE_HEADS, 2, HD], F32)
+            for h in range(ROPE_HEADS):
+                nc.vector.scalar_tensor_tensor(
+                    out=products[:, h, :, :],
+                    in0=banks[t][h].unsqueeze(1).to_broadcast([P, 2, HD]),
+                    scalar=rstd[:, h : h + 1],
+                    in1=rope_tables[t // CHUNK][:, t % CHUNK, h // Q_HEADS, :, :],
+                    op0=ALU.mult,
+                    op1=ALU.mult,
+                )
+            result = results[t // PAIR]
+            nc.gpsimd.tensor_tensor(
+                out=result[:, t % PAIR, 0:ROPE_HEADS, 0:HALF],
+                in0=products[:, :, 0, 0:HALF],
+                in1=products[:, :, 1, HALF:HD],
+                op=ALU.subtract,
+            )
+            nc.gpsimd.tensor_tensor(
+                out=result[:, t % PAIR, 0:ROPE_HEADS, HALF:HD],
+                in0=products[:, :, 0, HALF:HD],
+                in1=products[:, :, 1, 0:HALF],
+                op=ALU.add,
+            )
+            if t % PAIR == PAIR - 1:
+                rows = slice(t + 1 - PAIR, t + 1)
+                nc.sync.dma_start(
+                    out=q_dram[:, rows, :], in_=result[:, :, 0:Q_HEADS, :].rearrange("p t h d -> p t (h d)")
+                )
+                nc.sync.dma_start(out=k_dram[:, rows, :], in_=result[:, :, Q_HEADS, :])
+                nc.sync.dma_start(out=v_dram[:, rows, :], in_=result[:, :, ROPE_HEADS, :])
+
+        for i in range(TILES + 2):
+            if i < TILES:
+                quantise(i)
+            if 1 <= i <= TILES:
+                project(i - 1)
+                norms(i - 1)
+            if i >= 2:
+                rope(i - 2)

@@ -60,7 +60,7 @@ def tile_multiheadattention_pa_t_kernel(
 
     with ExitStack() as ctx:
         keep = ctx.enter_context(tc.tile_pool(name="keep", bufs=1))
-        tables = ctx.enter_context(tc.tile_pool(name="tables", bufs=2))
+        tables = ctx.enter_context(tc.tile_pool(name="tables", bufs=3))
         quant = ctx.enter_context(tc.tile_pool(name="quant", bufs=3))
         stats = ctx.enter_context(tc.tile_pool(name="stats", bufs=3))
         work = ctx.enter_context(tc.tile_pool(name="work", bufs=3))
@@ -73,6 +73,8 @@ def tile_multiheadattention_pa_t_kernel(
         nc.vector.memset(eps[:], EPS)
         ident = keep.tile([P, P], F32)
         make_identity(nc, ident[:])
+        ident_bf = keep.tile([P, P], BF16)
+        make_identity(nc, ident_bf[:])
 
         x_chunks = []
         cos_chunks = []
@@ -112,16 +114,32 @@ def tile_multiheadattention_pa_t_kernel(
         for c in range(1, TILES // CHUNK):
             load_chunk(c)
 
+        gain_diag = keep.tile([P, 2, 2, HD], BF16)
+        nc.gpsimd.tensor_tensor(
+            out=gain_diag[:, 0, :, :],
+            in0=ident_bf[:].unsqueeze(1).to_broadcast([P, 2, HD]),
+            in1=gains[:],
+            op=ALU.mult,
+        )
+        for mine, other in ((slice(0, HALF), slice(HALF, HD)), (slice(HALF, HD), slice(0, HALF))):
+            nc.gpsimd.tensor_tensor(
+                out=gain_diag[:, 1, :, mine],
+                in0=ident_bf[:, other].unsqueeze(1).to_broadcast([P, 2, HALF]),
+                in1=gains[:, :, mine],
+                op=ALU.mult,
+            )
+
         x_codes = {}
         x_scales = {}
         banks = {}
         rstds = {}
         rope_tables = {}
+        turned_chunks = {}
         results = {}
 
         def quantise(t):
             x_words = x_chunks[t // CHUNK][:, t % CHUNK, :].bitcast(F32)
-            xt = psum.tile([P, PASSES * 2, P], F32, tag="xt")
+            xt = psum.tile([P, PASSES * 2, P], F32, tag="xt", bufs=1)
             for g in range(PASSES):
                 for u in range(2):
                     nc.tensor.transpose(
@@ -165,48 +183,50 @@ def tile_multiheadattention_pa_t_kernel(
 
         def norms(t):
             if t % PAIR == 0:
-                result = work.tile([P, PAIR, OUT_HEADS, HD], F32, tag="result")
+                result = work.tile([P, PAIR, OUT_HEADS, HD], F32, tag="result", bufs=4)
                 results[t // PAIR] = result
             sumsq = stats.tile([P, ROPE_HEADS], F32)
             for h in range(ROPE_HEADS):
                 squares = stats.tile([P, HD], F32)
                 nc.scalar.activation(out=squares[:], in_=banks[t][h], func=ACT.Square, accum_out=sumsq[:, h : h + 1])
             nc.scalar.copy(out=results[t // PAIR][:, t % PAIR, ROPE_HEADS, :], in_=banks[t][ROPE_HEADS])
-            rms = stats.tile([P, ROPE_HEADS], F32)
-            nc.scalar.activation(out=rms[:], in_=sumsq[:], func=ACT.Sqrt, scale=1.0 / HD, bias=eps[:, 0:1])
-            rstds[t] = rms
-
-        def build_tables(c):
-            table = tables.tile([P, CHUNK, 2, 2, HD], F32)
-            shape = [P, CHUNK, 2, HD]
-            nc.vector.tensor_tensor(
-                out=table[:, :, :, 0, :],
-                in0=cos_chunks[c][:].unsqueeze(2).to_broadcast(shape),
-                in1=gains[:].unsqueeze(1).to_broadcast(shape),
-                op=ALU.mult,
+            rstd = stats.tile([P, ROPE_HEADS], F32)
+            nc.scalar.activation(
+                out=rstd[:], in_=sumsq[:], func=ACT.Abs_reciprocal_sqrt, scale=1.0 / HD, bias=eps[:, 0:1]
             )
-            shape = [P, CHUNK, 2, HALF]
-            for mine, other in ((slice(0, HALF), slice(HALF, HD)), (slice(HALF, HD), slice(0, HALF))):
-                nc.vector.tensor_tensor(
-                    out=table[:, :, :, 1, mine],
-                    in0=sin_chunks[c][:, :, other].unsqueeze(2).to_broadcast(shape),
-                    in1=gains[:, :, mine].unsqueeze(1).to_broadcast(shape),
-                    op=ALU.mult,
+            rstds[t] = rstd
+
+        def build_table(t):
+            c = t // CHUNK
+            if t % CHUNK == 0:
+                turned_ps = psum.tile([P, CHUNK, 2, P], BF16, tag="table", bufs=1)
+                for tt in range(CHUNK):
+                    nc.tensor.transpose(turned_ps[:, tt, 0, :], cos_chunks[c][:, tt, :], ident_bf[:])
+                    nc.tensor.transpose(turned_ps[:, tt, 1, :], sin_chunks[c][:, tt, :], ident_bf[:])
+                turned = tables.tile([P, CHUNK, 2, P], BF16)
+                nc.scalar.copy(out=turned[:], in_=turned_ps[:])
+                turned_chunks[c] = turned
+            table_ps = psum.tile([P, 2, 2 * HD], F32, tag="table", bufs=1)
+            for f in range(2):
+                nc.tensor.matmul(
+                    out=table_ps[:, f, :],
+                    lhsT=turned_chunks[c][:, t % CHUNK, f, :],
+                    rhs=gain_diag[:, f, :, :].rearrange("p m j -> p (m j)"),
+                    start=True,
+                    stop=True,
                 )
-            rope_tables[c] = table
+            table = tables.tile([P, 2, 2, HD], F32)
+            nc.scalar.copy(out=table[:].rearrange("p f m j -> p f (m j)"), in_=table_ps[:])
+            rope_tables[t] = table
 
         def rope(t):
-            if t % CHUNK == 0:
-                build_tables(t // CHUNK)
-            rstd = stats.tile([P, ROPE_HEADS], F32)
-            nc.vector.reciprocal(out=rstd[:], in_=rstds[t][:])
             products = work.tile([P, ROPE_HEADS, 2, HD], F32)
             for h in range(ROPE_HEADS):
                 nc.vector.scalar_tensor_tensor(
                     out=products[:, h, :, :],
                     in0=banks[t][h].unsqueeze(1).to_broadcast([P, 2, HD]),
-                    scalar=rstd[:, h : h + 1],
-                    in1=rope_tables[t // CHUNK][:, t % CHUNK, h // Q_HEADS, :, :],
+                    scalar=rstds[t][:, h : h + 1],
+                    in1=rope_tables[t][:, :, h // Q_HEADS, :],
                     op0=ALU.mult,
                     op1=ALU.mult,
                 )
@@ -235,6 +255,7 @@ def tile_multiheadattention_pa_t_kernel(
             if i < TILES:
                 quantise(i)
             if 1 <= i <= TILES:
+                build_table(i - 1)
                 project(i - 1)
                 norms(i - 1)
             if i >= 2:

@@ -25,8 +25,8 @@ N_ALL = OUT_HEADS * HD
 K_PASS = 512
 PASSES = D // K_PASS
 TILES = S // P
+X_CHUNK = 2
 CHUNK = 4
-PAIR = 2
 EPS = 1e-6
 
 FLOPS = 2 * S * D * N_ALL
@@ -63,7 +63,7 @@ def tile_multiheadattention_pa_t_kernel(
         tables = ctx.enter_context(tc.tile_pool(name="tables", bufs=3))
         quant = ctx.enter_context(tc.tile_pool(name="quant", bufs=3))
         stats = ctx.enter_context(tc.tile_pool(name="stats", bufs=3))
-        work = ctx.enter_context(tc.tile_pool(name="work", bufs=3))
+        work = ctx.enter_context(tc.tile_pool(name="work", bufs=4))
         psum = ctx.enter_context(tc.psum_pool(name="psum", bufs=2))
         ctx.enter_context(tc.manual_schedule())
 
@@ -76,43 +76,42 @@ def tile_multiheadattention_pa_t_kernel(
         ident_bf = keep.tile([P, P], BF16)
         make_identity(nc, ident_bf[:])
 
-        x_chunks = []
-        cos_chunks = []
-        sin_chunks = []
-        for c in range(TILES // CHUNK):
-            x_chunks.append(keep.tile([P, CHUNK, D], BF16, name="x%d" % c))
-            cos_chunks.append(keep.tile([P, CHUNK, HD], BF16, name="cos%d" % c))
-            sin_chunks.append(keep.tile([P, CHUNK, HD], BF16, name="sin%d" % c))
-
-        def load_chunk(c):
-            rows = slice(c * CHUNK, (c + 1) * CHUNK)
-            nc.sync.dma_start(out=x_chunks[c][:], in_=x_dram[:, rows, :])
-            nc.sync.dma_start(out=cos_chunks[c][:], in_=cos_dram[:, rows, :])
-            nc.sync.dma_start(out=sin_chunks[c][:], in_=sin_dram[:, rows, :])
-
-        load_chunk(0)
-
+        x_chunks = [keep.tile([P, X_CHUNK, D], BF16, name="x%d" % c) for c in range(TILES // X_CHUNK)]
+        cos_chunks = [keep.tile([P, CHUNK, HD], BF16, name="cos%d" % c) for c in range(TILES // CHUNK)]
+        sin_chunks = [keep.tile([P, CHUNK, HD], BF16, name="sin%d" % c) for c in range(TILES // CHUNK)]
         w_words = keep.tile([P, PASSES, 2 * N_ALL], U8, align_bytes=64)
-        col = 0
-        for words, scales in ((Wq_words, Wq_scales), (Wk_words, Wk_scales), (Wv_words, Wv_scales)):
+        gains = keep.tile([P, 2, HD], BF16)
+
+        def load_x(c):
+            nc.sync.dma_start(out=x_chunks[c][:], in_=x_dram[:, c * X_CHUNK : (c + 1) * X_CHUNK, :])
+
+        def load_cos_sin(c):
+            nc.sync.dma_start(out=cos_chunks[c][:], in_=cos_dram[:, c * CHUNK : (c + 1) * CHUNK, :])
+            nc.sync.dma_start(out=sin_chunks[c][:], in_=sin_dram[:, c * CHUNK : (c + 1) * CHUNK, :])
+
+        def load_weight(words, scales, first):
             width = scales.shape[2]
             nc.sync.dma_start(
-                out=w_words[:, :, 2 * col : 2 * (col + width)].bitcast(I32),
+                out=w_words[:, :, 2 * first : 2 * (first + width)].bitcast(I32),
                 in_=words.rearrange("g p b -> p g b").bitcast(I32),
             )
             for quad in range(4):
                 nc.sync.dma_start(
-                    out=w_scales[32 * quad : 32 * quad + 4, :, col : col + width].bitcast(I32),
+                    out=w_scales[32 * quad : 32 * quad + 4, :, first : first + width].bitcast(I32),
                     in_=scales[:, 4 * quad : 4 * quad + 4, :].rearrange("g r n -> r g n").bitcast(I32),
                 )
-            col += width
 
-        gains = keep.tile([P, 2, HD], BF16)
         nc.scalar.dma_start(out=gains[:, 0, :], in_=q_scale.partition_broadcast(P))
         nc.scalar.dma_start(out=gains[:, 1, :], in_=k_scale.partition_broadcast(P))
-
-        for c in range(1, TILES // CHUNK):
-            load_chunk(c)
+        load_x(0)
+        load_weight(Wq_words, Wq_scales, 0)
+        load_weight(Wk_words, Wk_scales, Q_HEADS * HD)
+        load_weight(Wv_words, Wv_scales, ROPE_HEADS * HD)
+        for c in range(TILES // CHUNK):
+            load_cos_sin(c)
+            for x_c in range(c * CHUNK // X_CHUNK, (c + 1) * CHUNK // X_CHUNK):
+                if x_c > 0:
+                    load_x(x_c)
 
         gain_diag = keep.tile([P, 2, 2, HD], BF16)
         nc.gpsimd.tensor_tensor(
@@ -135,10 +134,9 @@ def tile_multiheadattention_pa_t_kernel(
         rstds = {}
         rope_tables = {}
         turned_chunks = {}
-        results = {}
 
         def quantise(t):
-            x_words = x_chunks[t // CHUNK][:, t % CHUNK, :].bitcast(F32)
+            x_words = x_chunks[t // X_CHUNK][:, t % X_CHUNK, :].bitcast(F32)
             xt = psum.tile([P, PASSES * 2, P], F32, tag="xt", bufs=1)
             for g in range(PASSES):
                 for u in range(2):
@@ -182,14 +180,10 @@ def tile_multiheadattention_pa_t_kernel(
             banks[t] = [qa[:, h, :] for h in range(4)] + [qb[:, h, :] for h in range(4)] + [kv[:, 0, :], kv[:, 1, :]]
 
         def norms(t):
-            if t % PAIR == 0:
-                result = work.tile([P, PAIR, OUT_HEADS, HD], F32, tag="result", bufs=4)
-                results[t // PAIR] = result
             sumsq = stats.tile([P, ROPE_HEADS], F32)
             for h in range(ROPE_HEADS):
                 squares = stats.tile([P, HD], F32)
                 nc.scalar.activation(out=squares[:], in_=banks[t][h], func=ACT.Square, accum_out=sumsq[:, h : h + 1])
-            nc.scalar.copy(out=results[t // PAIR][:, t % PAIR, ROPE_HEADS, :], in_=banks[t][ROPE_HEADS])
             rstd = stats.tile([P, ROPE_HEADS], F32)
             nc.scalar.activation(
                 out=rstd[:], in_=sumsq[:], func=ACT.Abs_reciprocal_sqrt, scale=1.0 / HD, bias=eps[:, 0:1]
@@ -230,33 +224,30 @@ def tile_multiheadattention_pa_t_kernel(
                     op0=ALU.mult,
                     op1=ALU.mult,
                 )
-            result = results[t // PAIR]
+            result = work.tile([P, OUT_HEADS, HD], F32)
+            nc.vector.tensor_copy(out=result[:, ROPE_HEADS, :], in_=banks[t][ROPE_HEADS])
             nc.gpsimd.tensor_tensor(
-                out=result[:, t % PAIR, 0:ROPE_HEADS, 0:HALF],
+                out=result[:, 0:ROPE_HEADS, 0:HALF],
                 in0=products[:, :, 0, 0:HALF],
                 in1=products[:, :, 1, HALF:HD],
                 op=ALU.subtract,
             )
             nc.gpsimd.tensor_tensor(
-                out=result[:, t % PAIR, 0:ROPE_HEADS, HALF:HD],
+                out=result[:, 0:ROPE_HEADS, HALF:HD],
                 in0=products[:, :, 0, HALF:HD],
                 in1=products[:, :, 1, 0:HALF],
                 op=ALU.add,
             )
-            if t % PAIR == PAIR - 1:
-                rows = slice(t + 1 - PAIR, t + 1)
-                nc.sync.dma_start(
-                    out=q_dram[:, rows, :], in_=result[:, :, 0:Q_HEADS, :].rearrange("p t h d -> p t (h d)")
-                )
-                nc.sync.dma_start(out=k_dram[:, rows, :], in_=result[:, :, Q_HEADS, :])
-                nc.sync.dma_start(out=v_dram[:, rows, :], in_=result[:, :, ROPE_HEADS, :])
+            nc.sync.dma_start(out=q_dram[:, t, :], in_=result[:, 0:Q_HEADS, :].rearrange("p h d -> p (h d)"))
+            nc.sync.dma_start(out=k_dram[:, t, :], in_=result[:, Q_HEADS, :])
+            nc.sync.dma_start(out=v_dram[:, t, :], in_=result[:, ROPE_HEADS, :])
 
         for i in range(TILES + 2):
             if i < TILES:
                 quantise(i)
             if 1 <= i <= TILES:
-                build_table(i - 1)
                 project(i - 1)
                 norms(i - 1)
+                build_table(i - 1)
             if i >= 2:
                 rope(i - 2)

@@ -60,10 +60,10 @@ def tile_multiheadattention_pa_t_kernel(
 
     with ExitStack() as ctx:
         keep = ctx.enter_context(tc.tile_pool(name="keep", bufs=1))
-        tables = ctx.enter_context(tc.tile_pool(name="tables", bufs=3))
+        tables = ctx.enter_context(tc.tile_pool(name="tables", bufs=4))
         quant = ctx.enter_context(tc.tile_pool(name="quant", bufs=3))
         stats = ctx.enter_context(tc.tile_pool(name="stats", bufs=3))
-        work = ctx.enter_context(tc.tile_pool(name="work", bufs=4))
+        work = ctx.enter_context(tc.tile_pool(name="work", bufs=3))
         psum = ctx.enter_context(tc.psum_pool(name="psum", bufs=2))
         ctx.enter_context(tc.manual_schedule())
 
@@ -104,14 +104,14 @@ def tile_multiheadattention_pa_t_kernel(
         nc.scalar.dma_start(out=gains[:, 0, :], in_=q_scale.partition_broadcast(P))
         nc.scalar.dma_start(out=gains[:, 1, :], in_=k_scale.partition_broadcast(P))
         load_x(0)
+        load_cos_sin(0)
         load_weight(Wq_words, Wq_scales, 0)
         load_weight(Wk_words, Wk_scales, Q_HEADS * HD)
         load_weight(Wv_words, Wv_scales, ROPE_HEADS * HD)
-        for c in range(TILES // CHUNK):
-            load_cos_sin(c)
-            for x_c in range(c * CHUNK // X_CHUNK, (c + 1) * CHUNK // X_CHUNK):
-                if x_c > 0:
-                    load_x(x_c)
+        for x_c in range(1, TILES // X_CHUNK):
+            if (x_c * X_CHUNK) % CHUNK == 0:
+                load_cos_sin(x_c * X_CHUNK // CHUNK)
+            load_x(x_c)
 
         gain_diag = keep.tile([P, 2, 2, HD], BF16)
         nc.gpsimd.tensor_tensor(
@@ -128,14 +128,16 @@ def tile_multiheadattention_pa_t_kernel(
                 op=ALU.mult,
             )
 
+        x_grouped = {}
         x_codes = {}
         x_scales = {}
         banks = {}
         rstds = {}
         rope_tables = {}
+        results = {}
         turned_chunks = {}
 
-        def quantise(t):
+        def transpose_x(t):
             x_words = x_chunks[t // X_CHUNK][:, t % X_CHUNK, :].bitcast(F32)
             xt = psum.tile([P, PASSES * 2, P], F32, tag="xt", bufs=1)
             for g in range(PASSES):
@@ -145,12 +147,15 @@ def tile_multiheadattention_pa_t_kernel(
                     )
             grouped = quant.tile([P, PASSES, P, 2], F32, align_bytes=64)
             nc.scalar.copy(out=grouped[:], in_=xt[:].rearrange("p (g u) r -> p g r u", u=2))
+            x_grouped[t] = grouped
+
+        def quantise(t):
             codes = quant.tile([P, PASSES * P], U32, align_bytes=64)
             scales = quant.tile([P, PASSES * P], U8, align_bytes=64)
             nc.vector.quantize_mx(
                 out=codes[:].bitcast(FP8X4),
                 scales=scales[:],
-                in_=grouped[:].rearrange("p g r u -> p (g r u)").bitcast(BF16),
+                in_=x_grouped[t][:].rearrange("p g r u -> p (g r u)").bitcast(BF16),
             )
             x_codes[t] = codes
             x_scales[t] = scales
@@ -184,22 +189,26 @@ def tile_multiheadattention_pa_t_kernel(
             for h in range(ROPE_HEADS):
                 squares = stats.tile([P, HD], F32)
                 nc.scalar.activation(out=squares[:], in_=banks[t][h], func=ACT.Square, accum_out=sumsq[:, h : h + 1])
+            result = work.tile([P, OUT_HEADS, HD], F32, bufs=6)
+            nc.scalar.copy(out=result[:, ROPE_HEADS, :], in_=banks[t][ROPE_HEADS])
+            results[t] = result
             rstd = stats.tile([P, ROPE_HEADS], F32)
             nc.scalar.activation(
                 out=rstd[:], in_=sumsq[:], func=ACT.Abs_reciprocal_sqrt, scale=1.0 / HD, bias=eps[:, 0:1]
             )
             rstds[t] = rstd
 
+        def turn_cos_sin(c):
+            turned_ps = psum.tile([P, CHUNK, 2, P], BF16, tag="table", bufs=1)
+            for tt in range(CHUNK):
+                nc.tensor.transpose(turned_ps[:, tt, 0, :], cos_chunks[c][:, tt, :], ident_bf[:])
+                nc.tensor.transpose(turned_ps[:, tt, 1, :], sin_chunks[c][:, tt, :], ident_bf[:])
+            turned = tables.tile([P, CHUNK, 2, P], BF16, bufs=2)
+            nc.scalar.copy(out=turned[:], in_=turned_ps[:])
+            turned_chunks[c] = turned
+
         def build_table(t):
             c = t // CHUNK
-            if t % CHUNK == 0:
-                turned_ps = psum.tile([P, CHUNK, 2, P], BF16, tag="table", bufs=1)
-                for tt in range(CHUNK):
-                    nc.tensor.transpose(turned_ps[:, tt, 0, :], cos_chunks[c][:, tt, :], ident_bf[:])
-                    nc.tensor.transpose(turned_ps[:, tt, 1, :], sin_chunks[c][:, tt, :], ident_bf[:])
-                turned = tables.tile([P, CHUNK, 2, P], BF16)
-                nc.scalar.copy(out=turned[:], in_=turned_ps[:])
-                turned_chunks[c] = turned
             table_ps = psum.tile([P, 2, 2 * HD], F32, tag="table", bufs=1)
             for f in range(2):
                 nc.tensor.matmul(
@@ -224,8 +233,7 @@ def tile_multiheadattention_pa_t_kernel(
                     op0=ALU.mult,
                     op1=ALU.mult,
                 )
-            result = work.tile([P, OUT_HEADS, HD], F32)
-            nc.vector.tensor_copy(out=result[:, ROPE_HEADS, :], in_=banks[t][ROPE_HEADS])
+            result = results[t]
             nc.gpsimd.tensor_tensor(
                 out=result[:, 0:ROPE_HEADS, 0:HALF],
                 in0=products[:, :, 0, 0:HALF],
@@ -242,12 +250,18 @@ def tile_multiheadattention_pa_t_kernel(
             nc.sync.dma_start(out=k_dram[:, t, :], in_=result[:, Q_HEADS, :])
             nc.sync.dma_start(out=v_dram[:, t, :], in_=result[:, ROPE_HEADS, :])
 
+        transpose_x(0)
         for i in range(TILES + 2):
             if i < TILES:
                 quantise(i)
             if 1 <= i <= TILES:
                 project(i - 1)
                 norms(i - 1)
-                build_table(i - 1)
+            if i < TILES and i % CHUNK == 0:
+                turn_cos_sin(i // CHUNK)
+            if i + 1 < TILES:
+                transpose_x(i + 1)
+            if i < TILES:
+                build_table(i)
             if i >= 2:
                 rope(i - 2)

@@ -135,7 +135,9 @@ def tile_multiheadattention_pa_t_kernel(
         rstds = {}
         rope_tables = {}
         results = {}
-        turned_chunks = {}
+        product_tiles = {}
+        turned_banks = {}
+        turned_tiles = {}
 
         def transpose_x(t):
             x_words = x_chunks[t // X_CHUNK][:, t % X_CHUNK, :].bitcast(F32)
@@ -160,28 +162,40 @@ def tile_multiheadattention_pa_t_kernel(
             x_codes[t] = codes
             x_scales[t] = scales
 
+        def turn_cos_sin(t, quarter):
+            turned_ps = quarter.bitcast(BF16).rearrange("p (f s) -> p f s", f=2)
+            nc.tensor.transpose(turned_ps[:, 0, :], cos_chunks[t // CHUNK][:, t % CHUNK, :], ident_bf[:])
+            nc.tensor.transpose(turned_ps[:, 1, :], sin_chunks[t // CHUNK][:, t % CHUNK, :], ident_bf[:])
+            turned_banks[t] = turned_ps
+
+        def keep_turned(t):
+            turned = tables.tile([P, 2, P], BF16)
+            nc.scalar.copy(out=turned[:], in_=turned_banks[t])
+            turned_tiles[t] = turned
+
+        def mx_group(t, acc, first, width):
+            for g in range(PASSES):
+                tokens = slice(g * P, (g + 1) * P)
+                nc.tensor.matmul_mx(
+                    out=acc,
+                    lhsT=x_codes[t][:, tokens].bitcast(FP8X4),
+                    lhsT_scale=x_scales[t][:, tokens],
+                    rhs=w_words[:, g, 2 * first : 2 * (first + width)].bitcast(FP4X4),
+                    rhs_scale=w_scales[:, g, first : first + width],
+                    start=(g == 0),
+                    stop=(g == PASSES - 1),
+                )
+
         def project(t):
             qa = psum.tile([P, 4, HD], F32, tag="qa")
             qb = psum.tile([P, 4, HD], F32, tag="qb")
             kv = psum.tile([P, 4, HD], F32, tag="kv")
-            groups = (
-                (qa[:].rearrange("p h d -> p (h d)"), 0, 512),
-                (qb[:].rearrange("p h d -> p (h d)"), 512, 512),
-                (kv[:, 0, :], 1024, HD),
-                (kv[:, 1, :], 1152, HD),
-            )
-            for acc, first, width in groups:
-                for g in range(PASSES):
-                    tokens = slice(g * P, (g + 1) * P)
-                    nc.tensor.matmul_mx(
-                        out=acc,
-                        lhsT=x_codes[t][:, tokens].bitcast(FP8X4),
-                        lhsT_scale=x_scales[t][:, tokens],
-                        rhs=w_words[:, g, 2 * first : 2 * (first + width)].bitcast(FP4X4),
-                        rhs_scale=w_scales[:, g, first : first + width],
-                        start=(g == 0),
-                        stop=(g == PASSES - 1),
-                    )
+            mx_group(t, qa[:].rearrange("p h d -> p (h d)"), 0, 4 * HD)
+            mx_group(t, qb[:].rearrange("p h d -> p (h d)"), 4 * HD, 4 * HD)
+            if t + 2 < TILES:
+                turn_cos_sin(t + 2, kv[:, 2, :])
+            mx_group(t, kv[:, 0, :], Q_HEADS * HD, HD)
+            mx_group(t, kv[:, 1, :], ROPE_HEADS * HD, HD)
             banks[t] = [qa[:, h, :] for h in range(4)] + [qb[:, h, :] for h in range(4)] + [kv[:, 0, :], kv[:, 1, :]]
 
         def norms(t):
@@ -192,28 +206,20 @@ def tile_multiheadattention_pa_t_kernel(
             result = work.tile([P, OUT_HEADS, HD], F32, bufs=6)
             nc.scalar.copy(out=result[:, ROPE_HEADS, :], in_=banks[t][ROPE_HEADS])
             results[t] = result
+            if t + 2 < TILES:
+                keep_turned(t + 2)
             rstd = stats.tile([P, ROPE_HEADS], F32)
             nc.scalar.activation(
                 out=rstd[:], in_=sumsq[:], func=ACT.Abs_reciprocal_sqrt, scale=1.0 / HD, bias=eps[:, 0:1]
             )
             rstds[t] = rstd
 
-        def turn_cos_sin(c):
-            turned_ps = psum.tile([P, CHUNK, 2, P], BF16, tag="table", bufs=1)
-            for tt in range(CHUNK):
-                nc.tensor.transpose(turned_ps[:, tt, 0, :], cos_chunks[c][:, tt, :], ident_bf[:])
-                nc.tensor.transpose(turned_ps[:, tt, 1, :], sin_chunks[c][:, tt, :], ident_bf[:])
-            turned = tables.tile([P, CHUNK, 2, P], BF16, bufs=2)
-            nc.scalar.copy(out=turned[:], in_=turned_ps[:])
-            turned_chunks[c] = turned
-
         def build_table(t):
-            c = t // CHUNK
             table_ps = psum.tile([P, 2, 2 * HD], F32, tag="table", bufs=1)
             for f in range(2):
                 nc.tensor.matmul(
                     out=table_ps[:, f, :],
-                    lhsT=turned_chunks[c][:, t % CHUNK, f, :],
+                    lhsT=turned_tiles[t][:, f, :],
                     rhs=gain_diag[:, f, :, :].rearrange("p m j -> p (m j)"),
                     start=True,
                     stop=True,
@@ -222,17 +228,22 @@ def tile_multiheadattention_pa_t_kernel(
             nc.scalar.copy(out=table[:].rearrange("p f m j -> p f (m j)"), in_=table_ps[:])
             rope_tables[t] = table
 
-        def rope(t):
-            products = work.tile([P, ROPE_HEADS, 2, HD], F32)
-            for h in range(ROPE_HEADS):
+        def rope_products(t, first_head, end_head):
+            if first_head == 0:
+                products = work.tile([P, ROPE_HEADS, 2, HD], F32)
+                product_tiles[t] = products
+            for h in range(first_head, end_head):
                 nc.vector.scalar_tensor_tensor(
-                    out=products[:, h, :, :],
+                    out=product_tiles[t][:, h, :, :],
                     in0=banks[t][h].unsqueeze(1).to_broadcast([P, 2, HD]),
                     scalar=rstds[t][:, h : h + 1],
                     in1=rope_tables[t][:, :, h // Q_HEADS, :],
                     op0=ALU.mult,
                     op1=ALU.mult,
                 )
+
+        def rope_sums(t):
+            products = product_tiles[t]
             result = results[t]
             nc.gpsimd.tensor_tensor(
                 out=result[:, 0:ROPE_HEADS, 0:HALF],
@@ -251,17 +262,22 @@ def tile_multiheadattention_pa_t_kernel(
             nc.sync.dma_start(out=v_dram[:, t, :], in_=result[:, ROPE_HEADS, :])
 
         transpose_x(0)
+        first_turned = psum.tile([P, 4, HD], F32, tag="kv")
+        for t in range(2):
+            turn_cos_sin(t, first_turned[:, t, :])
+            keep_turned(t)
         for i in range(TILES + 2):
+            if i >= 2:
+                rope_products(i - 2, 0, 4)
             if i < TILES:
                 quantise(i)
             if 1 <= i <= TILES:
                 project(i - 1)
                 norms(i - 1)
-            if i < TILES and i % CHUNK == 0:
-                turn_cos_sin(i // CHUNK)
             if i + 1 < TILES:
                 transpose_x(i + 1)
             if i < TILES:
                 build_table(i)
             if i >= 2:
-                rope(i - 2)
+                rope_products(i - 2, 4, ROPE_HEADS)
+                rope_sums(i - 2)

@@ -127,6 +127,9 @@ def tile_multiheadattention_pa_t_kernel(
                 in1=gains[:, :, mine],
                 op=ALU.mult,
             )
+        nc.gpsimd.tensor_scalar_mul(
+            out=gain_diag[:, 1, :, HALF:HD], in0=gain_diag[:, 1, :, HALF:HD], scalar1=-1.0
+        )
 
         x_grouped = {}
         x_codes = {}
@@ -246,15 +249,9 @@ def tile_multiheadattention_pa_t_kernel(
             products = product_tiles[t]
             result = results[t]
             nc.gpsimd.tensor_tensor(
-                out=result[:, 0:ROPE_HEADS, 0:HALF],
-                in0=products[:, :, 0, 0:HALF],
-                in1=products[:, :, 1, HALF:HD],
-                op=ALU.subtract,
-            )
-            nc.gpsimd.tensor_tensor(
-                out=result[:, 0:ROPE_HEADS, HALF:HD],
-                in0=products[:, :, 0, HALF:HD],
-                in1=products[:, :, 1, 0:HALF],
+                out=result[:, 0:ROPE_HEADS, :].rearrange("p h (a d) -> p h a d", a=2),
+                in0=products[:, :, 0, :].rearrange("p h (a d) -> p h a d", a=2),
+                in1=products[:, :, 1, :].rearrange("p h (a d) -> p h a d", a=2)[:, :, ::-1, :],
                 op=ALU.add,
             )
             nc.sync.dma_start(out=q_dram[:, t, :], in_=result[:, 0:Q_HEADS, :].rearrange("p h d -> p (h d)"))

@@ -263,18 +263,18 @@ def tile_multiheadattention_pa_t_kernel(
         for t in range(2):
             turn_cos_sin(t, first_turned[:, t, :])
             keep_turned(t)
+        transpose_x(1)
         for i in range(TILES + 2):
-            if i >= 2:
-                rope_products(i - 2, 0, 4)
             if i < TILES:
                 quantise(i)
+            if i >= 2:
+                rope_products(i - 2, 0, ROPE_HEADS)
             if 1 <= i <= TILES:
                 project(i - 1)
                 norms(i - 1)
-            if i + 1 < TILES:
-                transpose_x(i + 1)
+            if i + 2 < TILES:
+                transpose_x(i + 2)
             if i < TILES:
                 build_table(i)
             if i >= 2:
-                rope_products(i - 2, 4, ROPE_HEADS)
                 rope_sums(i - 2)

@@ -28,6 +28,7 @@ TILES = S // P
 X_CHUNK = 2
 CHUNK = 4
 EPS = 1e-6
+EARLY = 4
 
 FLOPS = 2 * S * D * N_ALL
 
@@ -67,6 +68,8 @@ def tile_multiheadattention_pa_t_kernel(
         psum = ctx.enter_context(tc.psum_pool(name="psum", bufs=2))
         ctx.enter_context(tc.manual_schedule())
 
+        zeros = keep.tile([P, 4 * HD], BF16)
+        nc.vector.memset(zeros[:], 0.0)
         w_scales = keep.tile([P, PASSES, N_ALL], U8, align_bytes=64)
         nc.vector.memset(w_scales[:].rearrange("p g n -> p (g n)").bitcast(I32), 0)
         eps = keep.tile([P, 1], F32)
@@ -103,11 +106,15 @@ def tile_multiheadattention_pa_t_kernel(
 
         nc.scalar.dma_start(out=gains[:, 0, :], in_=q_scale.partition_broadcast(P))
         nc.scalar.dma_start(out=gains[:, 1, :], in_=k_scale.partition_broadcast(P))
-        load_x(0)
-        load_cos_sin(0)
+        nc.sync.dma_start(out=x_chunks[0][:, 0, :], in_=x_dram[:, 0, :])
+        nc.sync.dma_start(out=cos_chunks[0][:, 0:2, :], in_=cos_dram[:, 0:2, :])
+        nc.sync.dma_start(out=sin_chunks[0][:, 0:2, :], in_=sin_dram[:, 0:2, :])
+        nc.sync.dma_start(out=x_chunks[0][:, 1, :], in_=x_dram[:, 1, :])
         load_weight(Wq_words, Wq_scales, 0)
         load_weight(Wk_words, Wk_scales, Q_HEADS * HD)
         load_weight(Wv_words, Wv_scales, ROPE_HEADS * HD)
+        nc.sync.dma_start(out=cos_chunks[0][:, 2:CHUNK, :], in_=cos_dram[:, 2:CHUNK, :])
+        nc.sync.dma_start(out=sin_chunks[0][:, 2:CHUNK, :], in_=sin_dram[:, 2:CHUNK, :])
         for x_c in range(1, TILES // X_CHUNK):
             if (x_c * X_CHUNK) % CHUNK == 0:
                 load_cos_sin(x_c * X_CHUNK // CHUNK)
@@ -131,6 +138,7 @@ def tile_multiheadattention_pa_t_kernel(
             out=gain_diag[:, 1, :, HALF:HD], in0=gain_diag[:, 1, :, HALF:HD], scalar1=-1.0
         )
 
+        sumsqs = {}
         x_grouped = {}
         x_codes = {}
         x_scales = {}
@@ -144,7 +152,10 @@ def tile_multiheadattention_pa_t_kernel(
 
         def transpose_x(t):
             x_words = x_chunks[t // X_CHUNK][:, t % X_CHUNK, :].bitcast(F32)
-            xt = psum.tile([P, PASSES * 2, P], F32, tag="xt", bufs=1)
+            if t == 1:
+                xt = psum.tile([P, PASSES * 2, P], F32, tag="qa")
+            else:
+                xt = psum.tile([P, PASSES * 2, P], F32, tag="xt", bufs=1)
             for g in range(PASSES):
                 for u in range(2):
                     nc.tensor.transpose(
@@ -201,21 +212,30 @@ def tile_multiheadattention_pa_t_kernel(
             mx_group(t, kv[:, 1, :], ROPE_HEADS * HD, HD)
             banks[t] = [qa[:, h, :] for h in range(4)] + [qb[:, h, :] for h in range(4)] + [kv[:, 0, :], kv[:, 1, :]]
 
+        def take_rstd(t, first_head, end_head):
+            nc.scalar.activation(
+                out=rstds[t][:, first_head:end_head], in_=sumsqs[t][:, first_head:end_head],
+                func=ACT.Abs_reciprocal_sqrt, scale=1.0 / HD, bias=eps[:, 0:1],
+            )
+
         def norms(t):
             sumsq = stats.tile([P, ROPE_HEADS], F32)
+            sumsqs[t] = sumsq
+            rstd = stats.tile([P, ROPE_HEADS], F32)
+            rstds[t] = rstd
             for h in range(ROPE_HEADS):
                 squares = stats.tile([P, HD], F32)
                 nc.scalar.activation(out=squares[:], in_=banks[t][h], func=ACT.Square, accum_out=sumsq[:, h : h + 1])
+                if t == 0 and h == EARLY:
+                    take_rstd(t, 0, EARLY)
             result = work.tile([P, OUT_HEADS, HD], F32, bufs=6)
             nc.scalar.copy(out=result[:, ROPE_HEADS, :], in_=banks[t][ROPE_HEADS])
             results[t] = result
             if t + 2 < TILES:
                 keep_turned(t + 2)
-            rstd = stats.tile([P, ROPE_HEADS], F32)
-            nc.scalar.activation(
-                out=rstd[:], in_=sumsq[:], func=ACT.Abs_reciprocal_sqrt, scale=1.0 / HD, bias=eps[:, 0:1]
-            )
-            rstds[t] = rstd
+
+        def finish_norms(t):
+            take_rstd(t, EARLY if t == 0 else 0, ROPE_HEADS)
 
         def build_table(t):
             table_ps = psum.tile([P, 2, 2 * HD], F32, tag="table", bufs=1)
@@ -245,10 +265,10 @@ def tile_multiheadattention_pa_t_kernel(
                     op1=ALU.mult,
                 )
 
-        def rope_sums(t):
+        def rope_sums(engine, t):
             products = product_tiles[t]
             result = results[t]
-            nc.gpsimd.tensor_tensor(
+            engine.tensor_tensor(
                 out=result[:, 0:ROPE_HEADS, :].rearrange("p h (a d) -> p h a d", a=2),
                 in0=products[:, :, 0, :].rearrange("p h (a d) -> p h a d", a=2),
                 in1=products[:, :, 1, :].rearrange("p h (a d) -> p h a d", a=2)[:, :, ::-1, :],
@@ -258,23 +278,34 @@ def tile_multiheadattention_pa_t_kernel(
             nc.sync.dma_start(out=k_dram[:, t, :], in_=result[:, Q_HEADS, :])
             nc.sync.dma_start(out=v_dram[:, t, :], in_=result[:, ROPE_HEADS, :])
 
+        warm = psum.tile([P, 4 * HD], F32, tag="table", bufs=1)
+
+        def keep_warm(count):
+            for n in range(count):
+                nc.tensor.matmul(out=warm[:], lhsT=zeros[:, 0:P], rhs=zeros[:], start=True, stop=True)
+
+        keep_warm(4)
         transpose_x(0)
         first_turned = psum.tile([P, 4, HD], F32, tag="kv")
         for t in range(2):
             turn_cos_sin(t, first_turned[:, t, :])
             keep_turned(t)
-        transpose_x(1)
+        keep_warm(2)
         for i in range(TILES + 2):
+            if i == 2:
+                rope_products(0, 0, EARLY)
             if i < TILES:
                 quantise(i)
             if i >= 2:
-                rope_products(i - 2, 0, ROPE_HEADS)
+                rope_products(i - 2, EARLY if i == 2 else 0, ROPE_HEADS)
             if 1 <= i <= TILES:
                 project(i - 1)
                 norms(i - 1)
-            if i + 2 < TILES:
-                transpose_x(i + 2)
+            if i + 1 < TILES:
+                transpose_x(i + 1)
+            if 1 <= i <= TILES:
+                finish_norms(i - 1)
             if i < TILES:
                 build_table(i)
             if i >= 2:
-                rope_sums(i - 2)
+                rope_sums(nc.gpsimd if i <= TILES else nc.vector, i - 2)

@@ -248,7 +248,10 @@ def tile_multiheadattention_pa_t_kernel(
                     stop=True,
                 )
             table = tables.tile([P, 2, 2, HD], F32)
-            nc.scalar.copy(out=table[:].rearrange("p f m j -> p f (m j)"), in_=table_ps[:])
+            if t == 1:
+                nc.vector.tensor_copy(out=table[:].rearrange("p f m j -> p f (m j)"), in_=table_ps[:])
+            else:
+                nc.scalar.copy(out=table[:].rearrange("p f m j -> p f (m j)"), in_=table_ps[:])
             rope_tables[t] = table
 
         def rope_products(t, first_head, end_head):
@@ -291,6 +294,7 @@ def tile_multiheadattention_pa_t_kernel(
             turn_cos_sin(t, first_turned[:, t, :])
             keep_turned(t)
         keep_warm(2)
+        transpose_x(1)
         for i in range(TILES + 2):
             if i == 2:
                 rope_products(0, 0, EARLY)
@@ -301,11 +305,14 @@ def tile_multiheadattention_pa_t_kernel(
             if 1 <= i <= TILES:
                 project(i - 1)
                 norms(i - 1)
-            if i + 1 < TILES:
-                transpose_x(i + 1)
-            if 1 <= i <= TILES:
                 finish_norms(i - 1)
-            if i < TILES:
+            if i == 1:
+                build_table(1)
+                transpose_x(2)
+                transpose_x(3)
+            if i >= 2 and i + 2 < TILES:
+                transpose_x(i + 2)
+            if i < TILES and i != 1:
                 build_table(i)
             if i >= 2:
                 rope_sums(nc.gpsimd if i <= TILES else nc.vector, i - 2)

@@ -28,6 +28,7 @@ TILES = S // P
 X_CHUNK = 2
 CHUNK = 4
 EPS = 1e-6
+HEAD_TABLES = 6
 EARLY = 4
 
 FLOPS = 2 * S * D * N_ALL
@@ -107,18 +108,21 @@ def tile_multiheadattention_pa_t_kernel(
         nc.scalar.dma_start(out=gains[:, 0, :], in_=q_scale.partition_broadcast(P))
         nc.scalar.dma_start(out=gains[:, 1, :], in_=k_scale.partition_broadcast(P))
         nc.sync.dma_start(out=x_chunks[0][:, 0, :], in_=x_dram[:, 0, :])
-        nc.sync.dma_start(out=cos_chunks[0][:, 0:2, :], in_=cos_dram[:, 0:2, :])
-        nc.sync.dma_start(out=sin_chunks[0][:, 0:2, :], in_=sin_dram[:, 0:2, :])
         nc.sync.dma_start(out=x_chunks[0][:, 1, :], in_=x_dram[:, 1, :])
         load_weight(Wq_words, Wq_scales, 0)
         load_weight(Wk_words, Wk_scales, Q_HEADS * HD)
         load_weight(Wv_words, Wv_scales, ROPE_HEADS * HD)
-        nc.sync.dma_start(out=cos_chunks[0][:, 2:CHUNK, :], in_=cos_dram[:, 2:CHUNK, :])
-        nc.sync.dma_start(out=sin_chunks[0][:, 2:CHUNK, :], in_=sin_dram[:, 2:CHUNK, :])
+        load_cos_sin(0)
+        load_cos_sin(1)
         for x_c in range(1, TILES // X_CHUNK):
-            if (x_c * X_CHUNK) % CHUNK == 0:
+            if (x_c * X_CHUNK) % CHUNK == 0 and x_c * X_CHUNK // CHUNK > 1:
                 load_cos_sin(x_c * X_CHUNK // CHUNK)
             load_x(x_c)
+
+        signed_gains = keep.tile([P, 2, HD], BF16)
+        nc.gpsimd.tensor_scalar_mul(out=signed_gains[:, :, 0:HALF], in0=gains[:, :, 0:HALF], scalar1=1.0)
+        nc.gpsimd.tensor_scalar_mul(out=signed_gains[:, :, HALF:HD], in0=gains[:, :, HALF:HD], scalar1=-1.0)
+        head_tables = keep.tile([P, HEAD_TABLES, 2, 2, HD], F32)
 
         gain_diag = keep.tile([P, 2, 2, HD], BF16)
         nc.gpsimd.tensor_tensor(
@@ -206,7 +210,7 @@ def tile_multiheadattention_pa_t_kernel(
             kv = psum.tile([P, 4, HD], F32, tag="kv")
             mx_group(t, qa[:].rearrange("p h d -> p (h d)"), 0, 4 * HD)
             mx_group(t, qb[:].rearrange("p h d -> p (h d)"), 4 * HD, 4 * HD)
-            if t + 2 < TILES:
+            if HEAD_TABLES <= t + 2 < TILES:
                 turn_cos_sin(t + 2, kv[:, 2, :])
             mx_group(t, kv[:, 0, :], Q_HEADS * HD, HD)
             mx_group(t, kv[:, 1, :], ROPE_HEADS * HD, HD)
@@ -231,7 +235,7 @@ def tile_multiheadattention_pa_t_kernel(
             result = work.tile([P, OUT_HEADS, HD], F32, bufs=6)
             nc.scalar.copy(out=result[:, ROPE_HEADS, :], in_=banks[t][ROPE_HEADS])
             results[t] = result
-            if t + 2 < TILES:
+            if HEAD_TABLES <= t + 2 < TILES:
                 keep_turned(t + 2)
 
         def finish_norms(t):
@@ -248,11 +252,26 @@ def tile_multiheadattention_pa_t_kernel(
                     stop=True,
                 )
             table = tables.tile([P, 2, 2, HD], F32)
-            if t == 1:
-                nc.vector.tensor_copy(out=table[:].rearrange("p f m j -> p f (m j)"), in_=table_ps[:])
-            else:
-                nc.scalar.copy(out=table[:].rearrange("p f m j -> p f (m j)"), in_=table_ps[:])
+            nc.scalar.copy(out=table[:].rearrange("p f m j -> p f (m j)"), in_=table_ps[:])
             rope_tables[t] = table
+
+        def head_table(first, count):
+            tiles = slice(first % CHUNK, first % CHUNK + count)
+            nc.vector.tensor_tensor(
+                out=head_tables[:, first : first + count, 0, :, :],
+                in0=gains[:].unsqueeze(1).to_broadcast([P, count, 2, HD]),
+                in1=cos_chunks[first // CHUNK][:, tiles, :].unsqueeze(2).to_broadcast([P, count, 2, HD]),
+                op=ALU.mult,
+            )
+            for m in range(2):
+                nc.vector.tensor_tensor(
+                    out=head_tables[:, first : first + count, 1, m, :].rearrange("p t (a d) -> p t a d", a=2),
+                    in0=signed_gains[:, m, :].rearrange("p (a d) -> p a d", a=2).unsqueeze(1).to_broadcast([P, count, 2, HALF]),
+                    in1=sin_chunks[first // CHUNK][:, tiles, :].rearrange("p t (a d) -> p t a d", a=2)[:, :, ::-1, :],
+                    op=ALU.mult,
+                )
+            for t in range(first, first + count):
+                rope_tables[t] = head_tables[:, t, :, :, :]
 
         def rope_products(t, first_head, end_head):
             if first_head == 0:
@@ -289,10 +308,6 @@ def tile_multiheadattention_pa_t_kernel(
 
         keep_warm(4)
         transpose_x(0)
-        first_turned = psum.tile([P, 4, HD], F32, tag="kv")
-        for t in range(2):
-            turn_cos_sin(t, first_turned[:, t, :])
-            keep_turned(t)
         keep_warm(2)
         transpose_x(1)
         for i in range(TILES + 2):
@@ -300,6 +315,11 @@ def tile_multiheadattention_pa_t_kernel(
                 rope_products(0, 0, EARLY)
             if i < TILES:
                 quantise(i)
+            if i == 0:
+                head_table(0, 2)
+            if i == 1:
+                head_table(2, 2)
+                head_table(4, 2)
             if i >= 2:
                 rope_products(i - 2, EARLY if i == 2 else 0, ROPE_HEADS)
             if 1 <= i <= TILES:
@@ -307,12 +327,11 @@ def tile_multiheadattention_pa_t_kernel(
                 norms(i - 1)
                 finish_norms(i - 1)
             if i == 1:
-                build_table(1)
                 transpose_x(2)
                 transpose_x(3)
             if i >= 2 and i + 2 < TILES:
                 transpose_x(i + 2)
-            if i < TILES and i != 1:
+            if HEAD_TABLES <= i < TILES:
                 build_table(i)
             if i >= 2:
                 rope_sums(nc.gpsimd if i <= TILES else nc.vector, i - 2)

@@ -93,12 +93,14 @@ def tile_multiheadattention_pa_t_kernel(
             nc.sync.dma_start(out=cos_chunks[c][:], in_=cos_dram[:, c * CHUNK : (c + 1) * CHUNK, :])
             nc.sync.dma_start(out=sin_chunks[c][:], in_=sin_dram[:, c * CHUNK : (c + 1) * CHUNK, :])
 
-        def load_weight(words, scales, first):
-            width = scales.shape[2]
+        def load_words(words, first, width, skip=0):
             nc.sync.dma_start(
-                out=w_words[:, :, 2 * first : 2 * (first + width)].bitcast(I32),
-                in_=words.rearrange("g p b -> p g b").bitcast(I32),
+                out=w_words[:, :, 2 * (first + skip) : 2 * (first + skip + width)].bitcast(I32),
+                in_=words.rearrange("g p b -> p g b")[:, :, 2 * skip : 2 * (skip + width)].bitcast(I32),
             )
+
+        def load_scales(scales, first):
+            width = scales.shape[2]
             for quad in range(4):
                 nc.sync.dma_start(
                     out=w_scales[32 * quad : 32 * quad + 4, :, first : first + width].bitcast(I32),
@@ -108,10 +110,14 @@ def tile_multiheadattention_pa_t_kernel(
         nc.scalar.dma_start(out=gains[:, 0, :], in_=q_scale.partition_broadcast(P))
         nc.scalar.dma_start(out=gains[:, 1, :], in_=k_scale.partition_broadcast(P))
         nc.sync.dma_start(out=x_chunks[0][:, 0, :], in_=x_dram[:, 0, :])
+        load_scales(Wq_scales, 0)
+        load_scales(Wk_scales, Q_HEADS * HD)
+        load_scales(Wv_scales, ROPE_HEADS * HD)
+        load_words(Wq_words, 0, 4 * HD)
+        load_words(Wq_words, 0, 4 * HD, skip=4 * HD)
         nc.sync.dma_start(out=x_chunks[0][:, 1, :], in_=x_dram[:, 1, :])
-        load_weight(Wq_words, Wq_scales, 0)
-        load_weight(Wk_words, Wk_scales, Q_HEADS * HD)
-        load_weight(Wv_words, Wv_scales, ROPE_HEADS * HD)
+        load_words(Wk_words, Q_HEADS * HD, HD)
+        load_words(Wv_words, ROPE_HEADS * HD, HD)
         load_cos_sin(0)
         load_cos_sin(1)
         for x_c in range(1, TILES // X_CHUNK):

@@ -28,7 +28,7 @@ TILES = S // P
 X_CHUNK = 2
 CHUNK = 4
 EPS = 1e-6
-HEAD_TABLES = 6
+HEAD_TABLES = 2
 EARLY = 4
 
 FLOPS = 2 * S * D * N_ALL
@@ -69,10 +69,14 @@ def tile_multiheadattention_pa_t_kernel(
         psum = ctx.enter_context(tc.psum_pool(name="psum", bufs=2))
         ctx.enter_context(tc.manual_schedule())
 
+        gain_rows = keep.tile([P, 2 * HD], BF16)
+        nc.vector.memset(gain_rows[:], 0.0)
         zeros = keep.tile([P, 4 * HD], BF16)
         nc.vector.memset(zeros[:], 0.0)
         w_scales = keep.tile([P, PASSES, N_ALL], U8, align_bytes=64)
         nc.vector.memset(w_scales[:].rearrange("p g n -> p (g n)").bitcast(I32), 0)
+        ones = keep.tile([P, P], BF16)
+        nc.vector.memset(ones[:], 1.0)
         eps = keep.tile([P, 1], F32)
         nc.vector.memset(eps[:], EPS)
         ident = keep.tile([P, P], F32)
@@ -107,46 +111,59 @@ def tile_multiheadattention_pa_t_kernel(
                     in_=scales[:, 4 * quad : 4 * quad + 4, :].rearrange("g r n -> r g n").bitcast(I32),
                 )
 
-        nc.scalar.dma_start(out=gains[:, 0, :], in_=q_scale.partition_broadcast(P))
-        nc.scalar.dma_start(out=gains[:, 1, :], in_=k_scale.partition_broadcast(P))
+        nc.scalar.dma_start(out=gain_rows[0:1, 0:HD], in_=q_scale.unsqueeze(0))
+        nc.scalar.dma_start(out=gain_rows[0:1, HD : 2 * HD], in_=k_scale.unsqueeze(0))
         nc.sync.dma_start(out=x_chunks[0][:, 0, :], in_=x_dram[:, 0, :])
         load_scales(Wq_scales, 0)
         load_scales(Wk_scales, Q_HEADS * HD)
         load_scales(Wv_scales, ROPE_HEADS * HD)
         load_words(Wq_words, 0, 4 * HD)
-        load_words(Wq_words, 0, 4 * HD, skip=4 * HD)
+        nc.sync.dma_start(out=cos_chunks[0][:, 0:2, :], in_=cos_dram[:, 0:2, :])
+        nc.sync.dma_start(out=sin_chunks[0][:, 0:2, :], in_=sin_dram[:, 0:2, :])
         nc.sync.dma_start(out=x_chunks[0][:, 1, :], in_=x_dram[:, 1, :])
+        load_words(Wq_words, 0, 4 * HD, skip=4 * HD)
         load_words(Wk_words, Q_HEADS * HD, HD)
         load_words(Wv_words, ROPE_HEADS * HD, HD)
-        load_cos_sin(0)
-        load_cos_sin(1)
+        nc.sync.dma_start(out=cos_chunks[0][:, 2:CHUNK, :], in_=cos_dram[:, 2:CHUNK, :])
+        nc.sync.dma_start(out=sin_chunks[0][:, 2:CHUNK, :], in_=sin_dram[:, 2:CHUNK, :])
         for x_c in range(1, TILES // X_CHUNK):
-            if (x_c * X_CHUNK) % CHUNK == 0 and x_c * X_CHUNK // CHUNK > 1:
+            if (x_c * X_CHUNK) % CHUNK == 0:
                 load_cos_sin(x_c * X_CHUNK // CHUNK)
             load_x(x_c)
 
-        signed_gains = keep.tile([P, 2, HD], BF16)
-        nc.gpsimd.tensor_scalar_mul(out=signed_gains[:, :, 0:HALF], in0=gains[:, :, 0:HALF], scalar1=1.0)
-        nc.gpsimd.tensor_scalar_mul(out=signed_gains[:, :, HALF:HD], in0=gains[:, :, HALF:HD], scalar1=-1.0)
-        head_tables = keep.tile([P, HEAD_TABLES, 2, 2, HD], F32)
+        warm = psum.tile([P, 4 * HD], F32, tag="table", bufs=1)
 
+        def keep_warm(count):
+            for n in range(count):
+                nc.tensor.matmul(out=warm[:], lhsT=zeros[:, 0:P], rhs=zeros[:], start=True, stop=True)
+
+        keep_warm(4)
+        signed_gains = keep.tile([P, 2, HD], BF16)
+        head_tables = keep.tile([P, HEAD_TABLES, 2, 2, HD], F32)
         gain_diag = keep.tile([P, 2, 2, HD], BF16)
-        nc.gpsimd.tensor_tensor(
-            out=gain_diag[:, 0, :, :],
-            in0=ident_bf[:].unsqueeze(1).to_broadcast([P, 2, HD]),
-            in1=gains[:],
-            op=ALU.mult,
-        )
-        for mine, other in ((slice(0, HALF), slice(HALF, HD)), (slice(HALF, HD), slice(0, HALF))):
-            nc.gpsimd.tensor_tensor(
-                out=gain_diag[:, 1, :, mine],
-                in0=ident_bf[:, other].unsqueeze(1).to_broadcast([P, 2, HALF]),
-                in1=gains[:, :, mine],
+
+        def spread_gains():
+            spread = psum.tile([P, 4, HD], F32, tag="kv")
+            nc.tensor.matmul(
+                out=spread[:, 0:2, :].rearrange("p m j -> p (m j)"), lhsT=ones[:], rhs=gain_rows[:], start=True, stop=True
+            )
+            nc.vector.tensor_copy(out=gains[:], in_=spread[:, 0:2, :])
+            nc.vector.tensor_copy(out=signed_gains[:, :, 0:HALF], in_=gains[:, :, 0:HALF])
+            nc.vector.tensor_scalar_mul(out=signed_gains[:, :, HALF:HD], in0=gains[:, :, HALF:HD], scalar1=-1.0)
+
+        def build_gain_diag():
+            nc.vector.tensor_tensor(
+                out=gain_diag[:, 0, :, :],
+                in0=gains[:],
+                in1=ident_bf[:].unsqueeze(1).to_broadcast([P, 2, HD]),
                 op=ALU.mult,
             )
-        nc.gpsimd.tensor_scalar_mul(
-            out=gain_diag[:, 1, :, HALF:HD], in0=gain_diag[:, 1, :, HALF:HD], scalar1=-1.0
-        )
+            nc.vector.tensor_tensor(
+                out=gain_diag[:, 1, :, :].rearrange("p m (a d) -> p m a d", a=2),
+                in0=signed_gains[:].rearrange("p m (a d) -> p m a d", a=2),
+                in1=ident_bf[:].rearrange("p (a d) -> p a d", a=2)[:, ::-1, :].unsqueeze(1).to_broadcast([P, 2, 2, HALF]),
+                op=ALU.mult,
+            )
 
         sumsqs = {}
         x_grouped = {}
@@ -306,14 +323,8 @@ def tile_multiheadattention_pa_t_kernel(
             nc.sync.dma_start(out=k_dram[:, t, :], in_=result[:, Q_HEADS, :])
             nc.sync.dma_start(out=v_dram[:, t, :], in_=result[:, ROPE_HEADS, :])
 
-        warm = psum.tile([P, 4 * HD], F32, tag="table", bufs=1)
-
-        def keep_warm(count):
-            for n in range(count):
-                nc.tensor.matmul(out=warm[:], lhsT=zeros[:, 0:P], rhs=zeros[:], start=True, stop=True)
-
-        keep_warm(4)
         transpose_x(0)
+        spread_gains()
         keep_warm(2)
         transpose_x(1)
         for i in range(TILES + 2):
@@ -324,8 +335,7 @@ def tile_multiheadattention_pa_t_kernel(
             if i == 0:
                 head_table(0, 2)
             if i == 1:
-                head_table(2, 2)
-                head_table(4, 2)
+                build_gain_diag()
             if i >= 2:
                 rope_products(i - 2, EARLY if i == 2 else 0, ROPE_HEADS)
             if 1 <= i <= TILES:

@@ -171,7 +171,10 @@ def tile_multiheadattention_pa_t_kernel(
         x_scales = {}
         banks = {}
         rstds = {}
-        rope_tables = {}
+        q_tables = {}
+        k_tables = {}
+        k_inputs = {}
+        kv_banks = {}
         results = {}
         product_tiles = {}
         turned_banks = {}
@@ -237,6 +240,7 @@ def tile_multiheadattention_pa_t_kernel(
                 turn_cos_sin(t + 2, kv[:, 2, :])
             mx_group(t, kv[:, 0, :], Q_HEADS * HD, HD)
             mx_group(t, kv[:, 1, :], ROPE_HEADS * HD, HD)
+            kv_banks[t] = kv
             banks[t] = [qa[:, h, :] for h in range(4)] + [qb[:, h, :] for h in range(4)] + [kv[:, 0, :], kv[:, 1, :]]
 
         def take_rstd(t, first_head, end_head):
@@ -256,8 +260,9 @@ def tile_multiheadattention_pa_t_kernel(
                 if t == 0 and h == EARLY:
                     take_rstd(t, 0, EARLY)
             result = work.tile([P, OUT_HEADS, HD], F32, bufs=6)
-            nc.scalar.copy(out=result[:, ROPE_HEADS, :], in_=banks[t][ROPE_HEADS])
+            nc.scalar.copy(out=result[:, Q_HEADS:OUT_HEADS, :], in_=kv_banks[t][:, 0:2, :])
             results[t] = result
+            k_inputs[t] = banks[t][Q_HEADS] if t < HEAD_TABLES else result[:, Q_HEADS, :]
             if HEAD_TABLES <= t + 2 < TILES:
                 keep_turned(t + 2)
 
@@ -274,9 +279,10 @@ def tile_multiheadattention_pa_t_kernel(
                     start=True,
                     stop=True,
                 )
-            table = tables.tile([P, 2, 2, HD], F32)
-            nc.scalar.copy(out=table[:].rearrange("p f m j -> p f (m j)"), in_=table_ps[:])
-            rope_tables[t] = table
+            table = tables.tile([P, 2, HD], F32)
+            nc.scalar.copy(out=table[:], in_=table_ps[:, :, 0:HD])
+            q_tables[t] = table[:]
+            k_tables[t] = table_ps[:, :, HD : 2 * HD]
 
         def head_table(first, count):
             tiles = slice(first % CHUNK, first % CHUNK + count)
@@ -294,18 +300,19 @@ def tile_multiheadattention_pa_t_kernel(
                     op=ALU.mult,
                 )
             for t in range(first, first + count):
-                rope_tables[t] = head_tables[:, t, :, :, :]
+                q_tables[t] = head_tables[:, t, :, 0, :]
+                k_tables[t] = head_tables[:, t, :, 1, :]
 
-        def rope_products(t, first_head, end_head):
-            if first_head == 0:
+        def rope_products(t, heads):
+            if t not in product_tiles:
                 products = work.tile([P, ROPE_HEADS, 2, HD], F32)
                 product_tiles[t] = products
-            for h in range(first_head, end_head):
+            for h in heads:
                 nc.vector.scalar_tensor_tensor(
                     out=product_tiles[t][:, h, :, :],
-                    in0=banks[t][h].unsqueeze(1).to_broadcast([P, 2, HD]),
+                    in0=(banks[t][h] if h < Q_HEADS else k_inputs[t]).unsqueeze(1).to_broadcast([P, 2, HD]),
                     scalar=rstds[t][:, h : h + 1],
-                    in1=rope_tables[t][:, :, h // Q_HEADS, :],
+                    in1=q_tables[t] if h < Q_HEADS else k_tables[t],
                     op0=ALU.mult,
                     op1=ALU.mult,
                 )
@@ -329,15 +336,19 @@ def tile_multiheadattention_pa_t_kernel(
         transpose_x(1)
         for i in range(TILES + 2):
             if i == 2:
-                rope_products(0, 0, EARLY)
+                rope_products(0, range(0, EARLY))
             if i < TILES:
                 quantise(i)
             if i == 0:
                 head_table(0, 2)
             if i == 1:
                 build_gain_diag()
-            if i >= 2:
-                rope_products(i - 2, EARLY if i == 2 else 0, ROPE_HEADS)
+            if i == 2:
+                rope_products(0, range(EARLY, ROPE_HEADS))
+            if i == 3:
+                rope_products(1, range(0, ROPE_HEADS))
+            if i >= 4:
+                rope_products(i - 2, [Q_HEADS] + list(range(0, Q_HEADS)))
             if 1 <= i <= TILES:
                 project(i - 1)
                 norms(i - 1)
@@ -345,9 +356,9 @@ def tile_multiheadattention_pa_t_kernel(
             if i == 1:
                 transpose_x(2)
                 transpose_x(3)
+            if HEAD_TABLES <= i - 1 < TILES:
+                build_table(i - 1)
             if i >= 2 and i + 2 < TILES:
                 transpose_x(i + 2)
-            if HEAD_TABLES <= i < TILES:
-                build_table(i)
             if i >= 2:
                 rope_sums(nc.gpsimd if i <= TILES else nc.vector, i - 2)

from contextlib import ExitStack

import concourse.mybir as mybir
from concourse.masks import make_identity

F32 = mybir.dt.float32
BF16 = mybir.dt.bfloat16
I32 = mybir.dt.int32
U32 = mybir.dt.uint32
U8 = mybir.dt.uint8
FP8X4 = mybir.dt.float8_e4m3fn_x4
FP4X4 = mybir.dt.float4_e2m1fn_x4
ALU = mybir.AluOpType
ACT = mybir.ActivationFunctionType

P = 128
S = 4096
D = 1024
HD = 128
HALF = HD // 2
Q_HEADS = 8
ROPE_HEADS = Q_HEADS + 1
OUT_HEADS = ROPE_HEADS + 1
N_ALL = OUT_HEADS * HD
K_PASS = 512
PASSES = D // K_PASS
TILES = S // P
X_CHUNK = 2
CHUNK = 4
EPS = 1e-6
HEAD_TABLES = 2
EARLY = 4

FLOPS = 2 * S * D * N_ALL


def tile_multiheadattention_pa_t_kernel(
    tc,
    hidden_states,
    cos,
    sin,
    Wq_words,
    Wq_scales,
    Wk_words,
    Wk_scales,
    Wv_words,
    Wv_scales,
    q_scale,
    k_scale,
    out_0,
    out_1,
    out_2,
):
    nc = tc.nc

    x_dram = hidden_states.rearrange("b (p t) k -> (b p) t k", t=TILES)
    cos_dram = cos.rearrange("b (p t) d -> (b p) t d", t=TILES)
    sin_dram = sin.rearrange("b (p t) d -> (b p) t d", t=TILES)
    q_dram = out_0.rearrange("b (p t) h d -> (b p) t (h d)", t=TILES)
    k_dram = out_1.rearrange("b (p t) h d -> (b p) t (h d)", t=TILES)
    v_dram = out_2.rearrange("b (p t) h d -> (b p) t (h d)", t=TILES)

    with ExitStack() as ctx:
        keep = ctx.enter_context(tc.tile_pool(name="keep", bufs=1))
        tables = ctx.enter_context(tc.tile_pool(name="tables", bufs=4))
        quant = ctx.enter_context(tc.tile_pool(name="quant", bufs=3))
        stats = ctx.enter_context(tc.tile_pool(name="stats", bufs=3))
        work = ctx.enter_context(tc.tile_pool(name="work", bufs=3))
        psum = ctx.enter_context(tc.psum_pool(name="psum", bufs=2))
        ctx.enter_context(tc.manual_schedule())

        gain_rows = keep.tile([P, 2 * HD], BF16)
        nc.vector.memset(gain_rows[:], 0.0)
        zeros = keep.tile([P, 4 * HD], BF16)
        nc.vector.memset(zeros[:], 0.0)
        w_scales = keep.tile([P, PASSES, N_ALL], U8, align_bytes=64)
        nc.vector.memset(w_scales[:].rearrange("p g n -> p (g n)").bitcast(I32), 0)
        ones = keep.tile([P, P], BF16)
        nc.vector.memset(ones[:], 1.0)
        eps = keep.tile([P, 1], F32)
        nc.vector.memset(eps[:], EPS)
        ident = keep.tile([P, P], F32)
        make_identity(nc, ident[:])
        ident_bf = keep.tile([P, P], BF16)
        make_identity(nc, ident_bf[:])

        x_chunks = [keep.tile([P, X_CHUNK, D], BF16, name="x%d" % c) for c in range(TILES // X_CHUNK)]
        cos_chunks = [keep.tile([P, CHUNK, HD], BF16, name="cos%d" % c) for c in range(TILES // CHUNK)]
        sin_chunks = [keep.tile([P, CHUNK, HD], BF16, name="sin%d" % c) for c in range(TILES // CHUNK)]
        w_words = keep.tile([P, PASSES, 2 * N_ALL], U8, align_bytes=64)
        gains = keep.tile([P, 2, HD], BF16)

        def load_x(c):
            nc.sync.dma_start(out=x_chunks[c][:], in_=x_dram[:, c * X_CHUNK : (c + 1) * X_CHUNK, :])

        def load_cos_sin(c):
            nc.sync.dma_start(out=cos_chunks[c][:], in_=cos_dram[:, c * CHUNK : (c + 1) * CHUNK, :])
            nc.sync.dma_start(out=sin_chunks[c][:], in_=sin_dram[:, c * CHUNK : (c + 1) * CHUNK, :])

        def load_words(words, first, width, skip=0):
            nc.sync.dma_start(
                out=w_words[:, :, 2 * (first + skip) : 2 * (first + skip + width)].bitcast(I32),
                in_=words.rearrange("g p b -> p g b")[:, :, 2 * skip : 2 * (skip + width)].bitcast(I32),
            )

        def load_scales(scales, first):
            width = scales.shape[2]
            for quad in range(4):
                nc.sync.dma_start(
                    out=w_scales[32 * quad : 32 * quad + 4, :, first : first + width].bitcast(I32),
                    in_=scales[:, 4 * quad : 4 * quad + 4, :].rearrange("g r n -> r g n").bitcast(I32),
                )

        nc.scalar.dma_start(out=gain_rows[0:1, 0:HD], in_=q_scale.unsqueeze(0))
        nc.scalar.dma_start(out=gain_rows[0:1, HD : 2 * HD], in_=k_scale.unsqueeze(0))
        nc.sync.dma_start(out=x_chunks[0][:, 0, :], in_=x_dram[:, 0, :])
        load_scales(Wq_scales, 0)
        load_scales(Wk_scales, Q_HEADS * HD)
        load_scales(Wv_scales, ROPE_HEADS * HD)
        load_words(Wq_words, 0, 4 * HD)
        nc.sync.dma_start(out=cos_chunks[0][:, 0:2, :], in_=cos_dram[:, 0:2, :])
        nc.sync.dma_start(out=sin_chunks[0][:, 0:2, :], in_=sin_dram[:, 0:2, :])
        nc.sync.dma_start(out=x_chunks[0][:, 1, :], in_=x_dram[:, 1, :])
        load_words(Wq_words, 0, 4 * HD, skip=4 * HD)
        load_words(Wk_words, Q_HEADS * HD, HD)
        load_words(Wv_words, ROPE_HEADS * HD, HD)
        nc.sync.dma_start(out=cos_chunks[0][:, 2:CHUNK, :], in_=cos_dram[:, 2:CHUNK, :])
        nc.sync.dma_start(out=sin_chunks[0][:, 2:CHUNK, :], in_=sin_dram[:, 2:CHUNK, :])
        for x_c in range(1, TILES // X_CHUNK):
            if (x_c * X_CHUNK) % CHUNK == 0:
                load_cos_sin(x_c * X_CHUNK // CHUNK)
            load_x(x_c)

        warm = psum.tile([P, 4 * HD], F32, tag="table", bufs=1)

        def keep_warm(count):
            for n in range(count):
                nc.tensor.matmul(out=warm[:], lhsT=zeros[:, 0:P], rhs=zeros[:], start=True, stop=True)

        keep_warm(4)
        signed_gains = keep.tile([P, 2, HD], BF16)
        head_tables = keep.tile([P, HEAD_TABLES, 2, 2, HD], F32)
        gain_diag = keep.tile([P, 2, 2, HD], BF16)

        def spread_gains():
            spread = psum.tile([P, 4, HD], F32, tag="kv")
            nc.tensor.matmul(
                out=spread[:, 0:2, :].rearrange("p m j -> p (m j)"), lhsT=ones[:], rhs=gain_rows[:], start=True, stop=True
            )
            nc.vector.tensor_copy(out=gains[:], in_=spread[:, 0:2, :])
            nc.vector.tensor_copy(out=signed_gains[:, :, 0:HALF], in_=gains[:, :, 0:HALF])
            nc.vector.tensor_scalar_mul(out=signed_gains[:, :, HALF:HD], in0=gains[:, :, HALF:HD], scalar1=-1.0)

        def build_gain_diag():
            nc.vector.tensor_tensor(
                out=gain_diag[:, 0, :, :],
                in0=gains[:],
                in1=ident_bf[:].unsqueeze(1).to_broadcast([P, 2, HD]),
                op=ALU.mult,
            )
            nc.vector.tensor_tensor(
                out=gain_diag[:, 1, :, :].rearrange("p m (a d) -> p m a d", a=2),
                in0=signed_gains[:].rearrange("p m (a d) -> p m a d", a=2),
                in1=ident_bf[:].rearrange("p (a d) -> p a d", a=2)[:, ::-1, :].unsqueeze(1).to_broadcast([P, 2, 2, HALF]),
                op=ALU.mult,
            )

        sumsqs = {}
        x_grouped = {}
        x_codes = {}
        x_scales = {}
        banks = {}
        rstds = {}
        q_tables = {}
        k_tables = {}
        k_inputs = {}
        kv_banks = {}
        results = {}
        product_tiles = {}
        turned_banks = {}
        turned_tiles = {}

        def transpose_x(t):
            x_words = x_chunks[t // X_CHUNK][:, t % X_CHUNK, :].bitcast(F32)
            if t == 1:
                xt = psum.tile([P, PASSES * 2, P], F32, tag="qa")
            else:
                xt = psum.tile([P, PASSES * 2, P], F32, tag="xt", bufs=1)
            for g in range(PASSES):
                for u in range(2):
                    nc.tensor.transpose(
                        xt[:, 2 * g + u, :], x_words[:, 256 * g + u : 256 * (g + 1) : 2], ident[:]
                    )
            grouped = quant.tile([P, PASSES, P, 2], F32, align_bytes=64)
            nc.scalar.copy(out=grouped[:], in_=xt[:].rearrange("p (g u) r -> p g r u", u=2))
            x_grouped[t] = grouped

        def quantise(t):
            codes = quant.tile([P, PASSES * P], U32, align_bytes=64)
            scales = quant.tile([P, PASSES * P], U8, align_bytes=64)
            nc.vector.quantize_mx(
                out=codes[:].bitcast(FP8X4),
                scales=scales[:],
                in_=x_grouped[t][:].rearrange("p g r u -> p (g r u)").bitcast(BF16),
            )
            x_codes[t] = codes
            x_scales[t] = scales

        def turn_cos_sin(t, quarter):
            turned_ps = quarter.bitcast(BF16).rearrange("p (f s) -> p f s", f=2)
            nc.tensor.transpose(turned_ps[:, 0, :], cos_chunks[t // CHUNK][:, t % CHUNK, :], ident_bf[:])
            nc.tensor.transpose(turned_ps[:, 1, :], sin_chunks[t // CHUNK][:, t % CHUNK, :], ident_bf[:])
            turned_banks[t] = turned_ps

        def keep_turned(t):
            turned = tables.tile([P, 2, P], BF16)
            nc.scalar.copy(out=turned[:], in_=turned_banks[t])
            turned_tiles[t] = turned

        def mx_group(t, acc, first, width):
            for g in range(PASSES):
                tokens = slice(g * P, (g + 1) * P)
                nc.tensor.matmul_mx(
                    out=acc,
                    lhsT=x_codes[t][:, tokens].bitcast(FP8X4),
                    lhsT_scale=x_scales[t][:, tokens],
                    rhs=w_words[:, g, 2 * first : 2 * (first + width)].bitcast(FP4X4),
                    rhs_scale=w_scales[:, g, first : first + width],
                    start=(g == 0),
                    stop=(g == PASSES - 1),
                )

        def project(t):
            qa = psum.tile([P, 4, HD], F32, tag="qa")
            qb = psum.tile([P, 4, HD], F32, tag="qb")
            kv = psum.tile([P, 4, HD], F32, tag="kv")
            mx_group(t, qa[:].rearrange("p h d -> p (h d)"), 0, 4 * HD)
            mx_group(t, qb[:].rearrange("p h d -> p (h d)"), 4 * HD, 4 * HD)
            if HEAD_TABLES <= t + 2 < TILES:
                turn_cos_sin(t + 2, kv[:, 2, :])
            mx_group(t, kv[:, 0, :], Q_HEADS * HD, HD)
            mx_group(t, kv[:, 1, :], ROPE_HEADS * HD, HD)
            kv_banks[t] = kv
            banks[t] = [qa[:, h, :] for h in range(4)] + [qb[:, h, :] for h in range(4)] + [kv[:, 0, :], kv[:, 1, :]]

        def take_rstd(t, first_head, end_head):
            nc.scalar.activation(
                out=rstds[t][:, first_head:end_head], in_=sumsqs[t][:, first_head:end_head],
                func=ACT.Abs_reciprocal_sqrt, scale=1.0 / HD, bias=eps[:, 0:1],
            )

        def norms(t):
            sumsq = stats.tile([P, ROPE_HEADS], F32)
            sumsqs[t] = sumsq
            rstd = stats.tile([P, ROPE_HEADS], F32)
            rstds[t] = rstd
            for h in range(ROPE_HEADS):
                squares = stats.tile([P, HD], F32)
                nc.scalar.activation(out=squares[:], in_=banks[t][h], func=ACT.Square, accum_out=sumsq[:, h : h + 1])
                if t == 0 and h == EARLY:
                    take_rstd(t, 0, EARLY)
            result = work.tile([P, OUT_HEADS, HD], F32, bufs=6)
            nc.scalar.copy(out=result[:, Q_HEADS:OUT_HEADS, :], in_=kv_banks[t][:, 0:2, :])
            results[t] = result
            k_inputs[t] = banks[t][Q_HEADS] if t < HEAD_TABLES else result[:, Q_HEADS, :]
            if HEAD_TABLES <= t + 2 < TILES:
                keep_turned(t + 2)

        def finish_norms(t):
            take_rstd(t, EARLY if t == 0 else 0, ROPE_HEADS)

        def build_table(t):
            table_ps = psum.tile([P, 2, 2 * HD], F32, tag="table", bufs=1)
            for f in range(2):
                nc.tensor.matmul(
                    out=table_ps[:, f, :],
                    lhsT=turned_tiles[t][:, f, :],
                    rhs=gain_diag[:, f, :, :].rearrange("p m j -> p (m j)"),
                    start=True,
                    stop=True,
                )
            table = tables.tile([P, 2, HD], F32)
            nc.scalar.copy(out=table[:], in_=table_ps[:, :, 0:HD])
            q_tables[t] = table[:]
            k_tables[t] = table_ps[:, :, HD : 2 * HD]

        def head_table(first, count):
            tiles = slice(first % CHUNK, first % CHUNK + count)
            nc.vector.tensor_tensor(
                out=head_tables[:, first : first + count, 0, :, :],
                in0=gains[:].unsqueeze(1).to_broadcast([P, count, 2, HD]),
                in1=cos_chunks[first // CHUNK][:, tiles, :].unsqueeze(2).to_broadcast([P, count, 2, HD]),
                op=ALU.mult,
            )
            for m in range(2):
                nc.vector.tensor_tensor(
                    out=head_tables[:, first : first + count, 1, m, :].rearrange("p t (a d) -> p t a d", a=2),
                    in0=signed_gains[:, m, :].rearrange("p (a d) -> p a d", a=2).unsqueeze(1).to_broadcast([P, count, 2, HALF]),
                    in1=sin_chunks[first // CHUNK][:, tiles, :].rearrange("p t (a d) -> p t a d", a=2)[:, :, ::-1, :],
                    op=ALU.mult,
                )
            for t in range(first, first + count):
                q_tables[t] = head_tables[:, t, :, 0, :]
                k_tables[t] = head_tables[:, t, :, 1, :]

        def rope_products(t, heads):
            if t not in product_tiles:
                products = work.tile([P, ROPE_HEADS, 2, HD], F32)
                product_tiles[t] = products
            for h in heads:
                nc.vector.scalar_tensor_tensor(
                    out=product_tiles[t][:, h, :, :],
                    in0=(banks[t][h] if h < Q_HEADS else k_inputs[t]).unsqueeze(1).to_broadcast([P, 2, HD]),
                    scalar=rstds[t][:, h : h + 1],
                    in1=q_tables[t] if h < Q_HEADS else k_tables[t],
                    op0=ALU.mult,
                    op1=ALU.mult,
                )

        def rope_sums(engine, t):
            products = product_tiles[t]
            result = results[t]
            engine.tensor_tensor(
                out=result[:, 0:ROPE_HEADS, :].rearrange("p h (a d) -> p h a d", a=2),
                in0=products[:, :, 0, :].rearrange("p h (a d) -> p h a d", a=2),
                in1=products[:, :, 1, :].rearrange("p h (a d) -> p h a d", a=2)[:, :, ::-1, :],
                op=ALU.add,
            )
            nc.sync.dma_start(out=q_dram[:, t, :], in_=result[:, 0:Q_HEADS, :].rearrange("p h d -> p (h d)"))
            nc.sync.dma_start(out=k_dram[:, t, :], in_=result[:, Q_HEADS, :])
            nc.sync.dma_start(out=v_dram[:, t, :], in_=result[:, ROPE_HEADS, :])

        transpose_x(0)
        spread_gains()
        keep_warm(2)
        transpose_x(1)
        for i in range(TILES + 2):
            if i == 2:
                rope_products(0, range(0, EARLY))
            if i < TILES:
                quantise(i)
            if i == 0:
                head_table(0, 2)
            if i == 1:
                build_gain_diag()
            if i == 2:
                rope_products(0, range(EARLY, ROPE_HEADS))
            if i == 3:
                rope_products(1, range(0, ROPE_HEADS))
            if i >= 4:
                rope_products(i - 2, [Q_HEADS] + list(range(0, Q_HEADS)))
            if 1 <= i <= TILES:
                project(i - 1)
                norms(i - 1)
                finish_norms(i - 1)
            if i == 1:
                transpose_x(2)
                transpose_x(3)
            if HEAD_TABLES <= i - 1 < TILES:
                build_table(i - 1)
            if i >= 2 and i + 2 < TILES:
                transpose_x(i + 2)
            if i >= 2:
                rope_sums(nc.gpsimd if i <= TILES else nc.vector, i - 2)
